import numpy as np
import ml_dtypes

BF16 = ml_dtypes.bfloat16


def bf(x):
    return np.asarray(x, np.float32).astype(BF16)


def f32(x):
    return np.asarray(x, np.float32)


def f64(x):
    return np.asarray(x).astype(np.float64)


def striped(idx):
    return np.tile(idx.reshape(-1, 16).T, (8, 1))


C, S, N, D = 128, 1024, 128, 128
ANNEAL, SHIFT, NEAR = 0.1, 6.0, 100.0


def sigmoid(v):
    return 1.0 / (1.0 + np.exp(-v))


def setup_inputs():
    return {"content": bf(np.random.standard_normal((C, N, D))), "ctx": bf(0.05 * np.random.standard_normal((C, N, N))), "wg": bf(1.2 * np.random.standard_normal((D, N)) / np.sqrt(D)), "cw": f32(np.random.uniform(size=(C, S))), "offs": striped(np.random.permutation(S)[:N])}


def reference(content, ctx, wg, cw, offs):
    idx = offs[:16].T.reshape(-1)
    ct = f64(content)
    sims = np.maximum(ct.reshape(C * N, D) @ f64(wg), 0.0).sum(axis=1).reshape(C, N)
    scores = sigmoid(SHIFT - ANNEAL * sims) * (1.0 + np.arange(N) / NEAR)[None, :]
    weights = f64(cw)[:, idx] * scores + (1.0 - scores)
    cm = ct * weights[:, :, None]
    return cm.reshape(C * N, D).T @ f64(ctx).transpose(0, 2, 1).reshape(C * N, N)

@@ -1,0 +1,104 @@
+import concourse.mybir as mybir
+from concourse.masks import make_identity
+
+C, S, N, D = 128, 1024, 128, 128
+ANNEAL, SHIFT, NEAR = 0.1, 6.0, 100.0
+FLOPS = 2 * (2 * C * N * D * N)
+
+BF16, F32 = mybir.dt.bfloat16, mybir.dt.float32
+I32, U16 = mybir.dt.int32, mybir.dt.uint16
+ALU = mybir.AluOpType
+ACT = mybir.ActivationFunctionType
+
+GROUP = 8
+N_GROUPS = N // GROUP
+BANK_J = 4
+CTX_PARTS = 4
+
+
+def tile_weightedbackpacklmheadmodel_kernel(tc, content, ctx, wg, cw, offs, out):
+    nc = tc.nc
+    with (
+        tc.tile_pool(name="held", bufs=1) as held,
+        tc.tile_pool(name="flipped", bufs=3) as flipped,
+        tc.tile_pool(name="scratch", bufs=2) as scratch,
+        tc.tile_pool(name="scaled", bufs=8) as scaled,
+        tc.psum_pool(name="psum_flip", bufs=2) as psum_flip,
+        tc.psum_pool(name="psum_proj", bufs=4) as psum_proj,
+        tc.psum_pool(name="psum_out", bufs=1) as psum_out,
+    ):
+        offsets = held.tile([C, N // 16], U16, name="offsets")
+        nc.sync.dma_start(offsets[:], offs)
+        wg_sb = held.tile([D, N], BF16, name="wg_sb")
+        nc.scalar.dma_start(wg_sb[:], wg)
+        cw_sb = held.tile([C, S], F32, name="cw_sb")
+        nc.scalar.dma_start(cw_sb[:], cw)
+        content_sb = []
+        for g in range(N_GROUPS):
+            group_sb = held.tile([C, GROUP, D], BF16, name=f"content_sb{g}")
+            nc.sync.dma_start(group_sb[:], content[:, g * GROUP : (g + 1) * GROUP, :])
+            content_sb.append(group_sb)
+        ctx_sb = held.tile([C, N, N], BF16, name="ctx_sb")
+        rows = N // CTX_PARTS
+        for q in range(CTX_PARTS):
+            nc.sync.dma_start(ctx_sb[:, q * rows : (q + 1) * rows, :], ctx[:, q * rows : (q + 1) * rows, :])
+
+        ident_bf = held.tile([C, C], BF16, name="ident_bf")
+        make_identity(nc, ident_bf[:])
+        ident_f32 = held.tile([N, N], F32, name="ident_f32")
+        make_identity(nc, ident_f32[:])
+        position = held.tile([C, N], I32, name="position")
+        nc.gpsimd.iota(position[:], pattern=[[1, N]], base=0, channel_multiplier=0)
+        ramp = held.tile([C, N], F32, name="ramp")
+        nc.vector.tensor_scalar(ramp[:], position[:], 1.0 / NEAR, 1.0, ALU.mult, ALU.add)
+
+        sims = held.tile([C, N], F32, name="sims")
+
+        def flip(g):
+            flip_ps = psum_flip.tile([D, GROUP, C], BF16, name="flip_ps")
+            for k in range(GROUP):
+                nc.tensor.transpose(flip_ps[:, k, :], content_sb[g][:, k, :], ident_bf[:])
+            content_t = flipped.tile([D, GROUP, C], BF16, name="content_t")
+            nc.vector.tensor_copy(content_t[:], flip_ps[:])
+            return content_t
+
+        def project(g, content_t):
+            for b in range(GROUP // BANK_J):
+                proj_ps = psum_proj.tile([C, BANK_J, N], F32, name="proj_ps")
+                for k in range(BANK_J):
+                    nc.tensor.matmul(
+                        proj_ps[:, k, :], lhsT=content_t[:, b * BANK_J + k, :], rhs=wg_sb[:], start=True, stop=True
+                    )
+                for k in range(BANK_J):
+                    j = g * GROUP + b * BANK_J + k
+                    relu_out = scratch.tile([C, N], BF16, name="relu_out")
+                    nc.scalar.activation(relu_out[:], proj_ps[:, k, :], ACT.Relu, accum_out=sims[:, j : j + 1])
+
+        content_t = flip(0)
+        for g in range(N_GROUPS):
+            following_t = flip(g + 1) if g + 1 < N_GROUPS else None
+            project(g, content_t)
+            content_t = following_t
+
+        scores = held.tile([C, N], F32, name="scores")
+        nc.scalar.activation(scores[:], sims[:], ACT.Sigmoid, bias=SHIFT, scale=-ANNEAL)
+        nc.vector.tensor_tensor(scores[:], scores[:], ramp[:], ALU.mult)
+        picked = held.tile([C, N], F32, name="picked")
+        nc.vector.tensor_tensor(picked[:], cw_sb[:].indirect(offsets[:]), scores[:], ALU.mult)
+        weights = held.tile([C, N], F32, name="weights")
+        nc.vector.scalar_tensor_tensor(weights[:], picked[:], 1.0, scores[:], ALU.add, ALU.subtract)
+
+        acc_ps = psum_out.tile([N, D], F32, name="acc_ps")
+        for j in range(N):
+            g, k = divmod(j, GROUP)
+            weighted = scaled.tile([C, D], BF16, name="weighted")
+            nc.vector.tensor_scalar_mul(weighted[:], content_sb[g][:, k, :], weights[:, j : j + 1])
+            nc.tensor.matmul(acc_ps[:], lhsT=ctx_sb[:, :, j], rhs=weighted[:], start=(j == 0), stop=(j == N - 1))
+
+        acc_sb = held.tile([N, D], F32, name="acc_sb")
+        nc.vector.tensor_copy(acc_sb[:], acc_ps[:])
+        out_ps = psum_out.tile([D, N], F32, name="out_ps")
+        nc.tensor.transpose(out_ps[:], acc_sb[:], ident_f32[:])
+        out_sb = held.tile([D, N], F32, name="out_sb")
+        nc.vector.tensor_copy(out_sb[:], out_ps[:])
+        nc.sync.dma_start(out, out_sb[:])

@@ -13,6 +13,8 @@ ACT = mybir.ActivationFunctionType
 GROUP = 8
 N_GROUPS = N // GROUP
 BANK_J = 4
+N_BANKS = N // BANK_J
+BLOCK = 8
 CTX_PARTS = 4
 
 
@@ -52,7 +54,7 @@ def tile_weightedbackpacklmheadmodel_kernel(tc, content, ctx, wg, cw, offs, out)
         ramp = held.tile([C, N], F32, name="ramp")
         nc.vector.tensor_scalar(ramp[:], position[:], 1.0 / NEAR, 1.0, ALU.mult, ALU.add)
 
-        sims = held.tile([C, N], F32, name="sims")
+        sims = held.tile([C, N_BANKS, BLOCK], F32, name="sims")
 
         def flip(g):
             flip_ps = psum_flip.tile([D, GROUP, C], BF16, name="flip_ps")
@@ -64,15 +66,21 @@ def tile_weightedbackpacklmheadmodel_kernel(tc, content, ctx, wg, cw, offs, out)
 
         def project(g, content_t):
             for b in range(GROUP // BANK_J):
+                bank = g * (GROUP // BANK_J) + b
                 proj_ps = psum_proj.tile([C, BANK_J, N], F32, name="proj_ps")
                 for k in range(BANK_J):
                     nc.tensor.matmul(
                         proj_ps[:, k, :], lhsT=content_t[:, b * BANK_J + k, :], rhs=wg_sb[:], start=True, stop=True
                     )
                 for k in range(BANK_J):
-                    j = g * GROUP + b * BANK_J + k
-                    relu_out = scratch.tile([C, N], BF16, name="relu_out")
-                    nc.scalar.activation(relu_out[:], proj_ps[:, k, :], ACT.Relu, accum_out=sims[:, j : j + 1])
+                    if bank % 3 == 2:
+                        relu_v = scratch.tile([C, N], BF16, name="relu_v")
+                        nc.vector.tensor_scalar(
+                            relu_v[:], proj_ps[:, k, :], 0.0, None, ALU.max, ALU.add, accum_out=sims[:, bank, k : k + 1]
+                        )
+                    else:
+                        relu_s = scratch.tile([C, N], BF16, name="relu_s")
+                        nc.scalar.activation(relu_s[:], proj_ps[:, k, :], ACT.Relu, accum_out=sims[:, bank, k : k + 1])
 
         content_t = flip(0)
         for g in range(N_GROUPS):
@@ -81,7 +89,9 @@ def tile_weightedbackpacklmheadmodel_kernel(tc, content, ctx, wg, cw, offs, out)
             content_t = following_t
 
         scores = held.tile([C, N], F32, name="scores")
-        nc.scalar.activation(scores[:], sims[:], ACT.Sigmoid, bias=SHIFT, scale=-ANNEAL)
+        nc.scalar.activation(
+            scores[:].rearrange("c (b k) -> c b k", k=BANK_J), sims[:, :, 0:BANK_J], ACT.Sigmoid, bias=SHIFT, scale=-ANNEAL
+        )
         nc.vector.tensor_tensor(scores[:], scores[:], ramp[:], ALU.mult)
         picked = held.tile([C, N], F32, name="picked")
         nc.vector.tensor_tensor(picked[:], cw_sb[:].indirect(offsets[:]), scores[:], ALU.mult)

@@ -15,6 +15,7 @@ N_GROUPS = N // GROUP
 BANK_J = 4
 N_BANKS = N // BANK_J
 BLOCK = 8
+HALF = N // 2
 CTX_PARTS = 4
 
 
@@ -54,7 +55,8 @@ def tile_weightedbackpacklmheadmodel_kernel(tc, content, ctx, wg, cw, offs, out)
         ramp = held.tile([C, N], F32, name="ramp")
         nc.vector.tensor_scalar(ramp[:], position[:], 1.0 / NEAR, 1.0, ALU.mult, ALU.add)
 
-        sims = held.tile([C, N_BANKS, BLOCK], F32, name="sims")
+        sims = [held.tile([C, HALF // BANK_J, BLOCK], F32, name=f"sims{h}") for h in range(2)]
+        weights = [held.tile([C, HALF], F32, name=f"weights{h}") for h in range(2)]
 
         def flip(g):
             flip_ps = psum_flip.tile([D, GROUP, C], BF16, name="flip_ps")
@@ -67,6 +69,7 @@ def tile_weightedbackpacklmheadmodel_kernel(tc, content, ctx, wg, cw, offs, out)
         def project(g, content_t):
             for b in range(GROUP // BANK_J):
                 bank = g * (GROUP // BANK_J) + b
+                h, bank_h = divmod(bank, HALF // BANK_J)
                 proj_ps = psum_proj.tile([C, BANK_J, N], F32, name="proj_ps")
                 for k in range(BANK_J):
                     nc.tensor.matmul(
@@ -76,33 +79,43 @@ def tile_weightedbackpacklmheadmodel_kernel(tc, content, ctx, wg, cw, offs, out)
                     if bank % 3 == 2:
                         relu_v = scratch.tile([C, N], BF16, name="relu_v")
                         nc.vector.tensor_scalar(
-                            relu_v[:], proj_ps[:, k, :], 0.0, None, ALU.max, ALU.add, accum_out=sims[:, bank, k : k + 1]
+                            relu_v[:], proj_ps[:, k, :], 0.0, None, ALU.max, ALU.add, accum_out=sims[h][:, bank_h, k : k + 1]
                         )
                     else:
                         relu_s = scratch.tile([C, N], BF16, name="relu_s")
-                        nc.scalar.activation(relu_s[:], proj_ps[:, k, :], ACT.Relu, accum_out=sims[:, bank, k : k + 1])
+                        nc.scalar.activation(
+                            relu_s[:], proj_ps[:, k, :], ACT.Relu, accum_out=sims[h][:, bank_h, k : k + 1]
+                        )
+
+        def weigh(h):
+            scores = held.tile([C, HALF], F32, name=f"scores{h}")
+            nc.scalar.activation(
+                scores[:].rearrange("c (b k) -> c b k", k=BANK_J),
+                sims[h][:, :, 0:BANK_J],
+                ACT.Sigmoid,
+                bias=SHIFT,
+                scale=-ANNEAL,
+            )
+            nc.vector.tensor_tensor(scores[:], scores[:], ramp[:, h * HALF : (h + 1) * HALF], ALU.mult)
+            picked = held.tile([C, HALF], F32, name=f"picked{h}")
+            half_of_list = offsets[:, h * (HALF // 16) : (h + 1) * (HALF // 16)]
+            nc.vector.tensor_tensor(picked[:], cw_sb[:].indirect(half_of_list), scores[:], ALU.mult)
+            nc.vector.scalar_tensor_tensor(weights[h][:], picked[:], 1.0, scores[:], ALU.add, ALU.subtract)
 
         content_t = flip(0)
         for g in range(N_GROUPS):
             following_t = flip(g + 1) if g + 1 < N_GROUPS else None
             project(g, content_t)
             content_t = following_t
-
-        scores = held.tile([C, N], F32, name="scores")
-        nc.scalar.activation(
-            scores[:].rearrange("c (b k) -> c b k", k=BANK_J), sims[:, :, 0:BANK_J], ACT.Sigmoid, bias=SHIFT, scale=-ANNEAL
-        )
-        nc.vector.tensor_tensor(scores[:], scores[:], ramp[:], ALU.mult)
-        picked = held.tile([C, N], F32, name="picked")
-        nc.vector.tensor_tensor(picked[:], cw_sb[:].indirect(offsets[:]), scores[:], ALU.mult)
-        weights = held.tile([C, N], F32, name="weights")
-        nc.vector.scalar_tensor_tensor(weights[:], picked[:], 1.0, scores[:], ALU.add, ALU.subtract)
+            if (g + 1) * GROUP % HALF == 0:
+                weigh((g + 1) * GROUP // HALF - 1)
 
         acc_ps = psum_out.tile([N, D], F32, name="acc_ps")
         for j in range(N):
             g, k = divmod(j, GROUP)
+            h, j_h = divmod(j, HALF)
             weighted = scaled.tile([C, D], BF16, name="weighted")
-            nc.vector.tensor_scalar_mul(weighted[:], content_sb[g][:, k, :], weights[:, j : j + 1])
+            nc.vector.tensor_scalar_mul(weighted[:], content_sb[g][:, k, :], weights[h][:, j_h : j_h + 1])
             nc.tensor.matmul(acc_ps[:], lhsT=ctx_sb[:, :, j], rhs=weighted[:], start=(j == 0), stop=(j == N - 1))
 
         acc_sb = held.tile([N, D], F32, name="acc_sb")

@@ -16,6 +16,7 @@ BANK_J = 4
 N_BANKS = N // BANK_J
 BLOCK = 8
 HALF = N // 2
+AHEAD = 2
 CTX_PARTS = 4
 
 
@@ -23,10 +24,10 @@ def tile_weightedbackpacklmheadmodel_kernel(tc, content, ctx, wg, cw, offs, out)
     nc = tc.nc
     with (
         tc.tile_pool(name="held", bufs=1) as held,
-        tc.tile_pool(name="flipped", bufs=3) as flipped,
+        tc.tile_pool(name="flipped", bufs=4) as flipped,
         tc.tile_pool(name="scratch", bufs=2) as scratch,
         tc.tile_pool(name="scaled", bufs=8) as scaled,
-        tc.psum_pool(name="psum_flip", bufs=2) as psum_flip,
+        tc.psum_pool(name="psum_flip", bufs=3) as psum_flip,
         tc.psum_pool(name="psum_proj", bufs=4) as psum_proj,
         tc.psum_pool(name="psum_out", bufs=1) as psum_out,
     ):
@@ -61,7 +62,7 @@ def tile_weightedbackpacklmheadmodel_kernel(tc, content, ctx, wg, cw, offs, out)
         def flip(g):
             flip_ps = psum_flip.tile([D, GROUP, C], BF16, name="flip_ps")
             for k in range(GROUP):
-                nc.tensor.transpose(flip_ps[:, k, :], content_sb[g][:, k, :], ident_bf[:])
+                nc.tensor.matmul(flip_ps[:, k, :], lhsT=content_sb[g][:, k, :], rhs=ident_bf[:], start=True, stop=True)
             content_t = flipped.tile([D, GROUP, C], BF16, name="content_t")
             nc.vector.tensor_copy(content_t[:], flip_ps[:])
             return content_t
@@ -102,11 +103,11 @@ def tile_weightedbackpacklmheadmodel_kernel(tc, content, ctx, wg, cw, offs, out)
             nc.vector.tensor_tensor(picked[:], cw_sb[:].indirect(half_of_list), scores[:], ALU.mult)
             nc.vector.scalar_tensor_tensor(weights[h][:], picked[:], 1.0, scores[:], ALU.add, ALU.subtract)
 
-        content_t = flip(0)
+        content_t = [flip(g) for g in range(AHEAD)]
         for g in range(N_GROUPS):
-            following_t = flip(g + 1) if g + 1 < N_GROUPS else None
-            project(g, content_t)
-            content_t = following_t
+            if g + AHEAD < N_GROUPS:
+                content_t.append(flip(g + AHEAD))
+            project(g, content_t[g])
             if (g + 1) * GROUP % HALF == 0:
                 weigh((g + 1) * GROUP // HALF - 1)
 
@@ -120,7 +121,7 @@ def tile_weightedbackpacklmheadmodel_kernel(tc, content, ctx, wg, cw, offs, out)
 
         acc_sb = held.tile([N, D], F32, name="acc_sb")
         nc.vector.tensor_copy(acc_sb[:], acc_ps[:])
-        out_ps = psum_out.tile([D, N], F32, name="out_ps")
+        out_ps = psum_flip.tile([D, N], F32, name="out_ps", tag="flip_ps")
         nc.tensor.transpose(out_ps[:], acc_sb[:], ident_f32[:])
         out_sb = held.tile([D, N], F32, name="out_sb")
         nc.vector.tensor_copy(out_sb[:], out_ps[:])

@@ -13,10 +13,10 @@ ACT = mybir.ActivationFunctionType
 GROUP = 8
 N_GROUPS = N // GROUP
 BANK_J = 4
-N_BANKS = N // BANK_J
 BLOCK = 8
 HALF = N // 2
 AHEAD = 2
+WARM_UP = 16
 CTX_PARTS = 4
 
 
@@ -24,12 +24,11 @@ def tile_weightedbackpacklmheadmodel_kernel(tc, content, ctx, wg, cw, offs, out)
     nc = tc.nc
     with (
         tc.tile_pool(name="held", bufs=1) as held,
-        tc.tile_pool(name="flipped", bufs=4) as flipped,
+        tc.tile_pool(name="flipped", bufs=AHEAD + 2) as flipped,
         tc.tile_pool(name="scratch", bufs=2) as scratch,
-        tc.tile_pool(name="scaled", bufs=8) as scaled,
-        tc.psum_pool(name="psum_flip", bufs=3) as psum_flip,
-        tc.psum_pool(name="psum_proj", bufs=4) as psum_proj,
-        tc.psum_pool(name="psum_out", bufs=1) as psum_out,
+        tc.tile_pool(name="scaled", bufs=GROUP) as scaled,
+        tc.psum_pool(name="psum_flip", bufs=2) as psum_flip,
+        tc.psum_pool(name="psum_proj", bufs=6) as psum_proj,
     ):
         offsets = held.tile([C, N // 16], U16, name="offsets")
         nc.sync.dma_start(offsets[:], offs)
@@ -55,6 +54,10 @@ def tile_weightedbackpacklmheadmodel_kernel(tc, content, ctx, wg, cw, offs, out)
         nc.gpsimd.iota(position[:], pattern=[[1, N]], base=0, channel_multiplier=0)
         ramp = held.tile([C, N], F32, name="ramp")
         nc.vector.tensor_scalar(ramp[:], position[:], 1.0 / NEAR, 1.0, ALU.mult, ALU.add)
+
+        warm_ps = psum_proj.tile([C, BANK_J, N], F32, name="warm_ps", tag="proj_ps")
+        for w in range(WARM_UP):
+            nc.tensor.matmul(warm_ps[:, w % BANK_J, :], lhsT=ident_bf[:], rhs=ident_bf[:], start=True, stop=True)
 
         sims = [held.tile([C, HALF // BANK_J, BLOCK], F32, name=f"sims{h}") for h in range(2)]
         weights = [held.tile([C, HALF], F32, name=f"weights{h}") for h in range(2)]
@@ -111,7 +114,7 @@ def tile_weightedbackpacklmheadmodel_kernel(tc, content, ctx, wg, cw, offs, out)
             if (g + 1) * GROUP % HALF == 0:
                 weigh((g + 1) * GROUP // HALF - 1)
 
-        acc_ps = psum_out.tile([N, D], F32, name="acc_ps")
+        acc_ps = psum_proj.tile([N, D], F32, name="acc_ps", tag="proj_ps")
         for j in range(N):
             g, k = divmod(j, GROUP)
             h, j_h = divmod(j, HALF)

@@ -55,6 +55,11 @@ def tile_weightedbackpacklmheadmodel_kernel(tc, content, ctx, wg, cw, offs, out)
         ramp = held.tile([C, N], F32, name="ramp")
         nc.vector.tensor_scalar(ramp[:], position[:], 1.0 / NEAR, 1.0, ALU.mult, ALU.add)
 
+        table_in = held.tile([C, 1], F32, name="table_in")
+        nc.vector.memset(table_in[:], 0.0)
+        table_out = held.tile([C, 1], F32, name="table_out")
+        nc.scalar.activation(table_out[:], table_in[:], ACT.Sigmoid)
+
         warm_ps = psum_proj.tile([C, BANK_J, N], F32, name="warm_ps", tag="proj_ps")
         for w in range(WARM_UP):
             nc.tensor.matmul(warm_ps[:, w % BANK_J, :], lhsT=ident_bf[:], rhs=ident_bf[:], start=True, stop=True)

@@ -70,7 +70,7 @@ def tile_weightedbackpacklmheadmodel_kernel(tc, content, ctx, wg, cw, offs, out)
         def flip(g):
             flip_ps = psum_flip.tile([D, GROUP, C], BF16, name="flip_ps")
             for k in range(GROUP):
-                nc.tensor.matmul(flip_ps[:, k, :], lhsT=content_sb[g][:, k, :], rhs=ident_bf[:], start=True, stop=True)
+                nc.tensor.transpose(flip_ps[:, k, :], content_sb[g][:, k, :], ident_bf[:])
             content_t = flipped.tile([D, GROUP, C], BF16, name="content_t")
             nc.vector.tensor_copy(content_t[:], flip_ps[:])
             return content_t

@@ -16,6 +16,8 @@ BANK_J = 4
 BLOCK = 8
 HALF = N // 2
 AHEAD = 2
+MIX_FROM = 14
+MIX_RATE = 1
 WARM_UP = 16
 CTX_PARTS = 4
 
@@ -26,18 +28,20 @@ def tile_weightedbackpacklmheadmodel_kernel(tc, content, ctx, wg, cw, offs, out)
         tc.tile_pool(name="held", bufs=1) as held,
         tc.tile_pool(name="flipped", bufs=AHEAD + 2) as flipped,
         tc.tile_pool(name="scratch", bufs=2) as scratch,
-        tc.tile_pool(name="scaled", bufs=GROUP) as scaled,
+        tc.tile_pool(name="scaled", bufs=2 * GROUP) as scaled,
         tc.psum_pool(name="psum_flip", bufs=2) as psum_flip,
-        tc.psum_pool(name="psum_proj", bufs=6) as psum_proj,
+        tc.psum_pool(name="psum_proj", bufs=5) as psum_proj,
+        tc.psum_pool(name="psum_acc", bufs=1) as psum_acc,
     ):
         offsets = held.tile([C, N // 16], U16, name="offsets")
         nc.sync.dma_start(offsets[:], offs)
         wg_sb = held.tile([D, N], BF16, name="wg_sb")
         nc.scalar.dma_start(wg_sb[:], wg)
         cw_sb = held.tile([C, S], F32, name="cw_sb")
-        nc.scalar.dma_start(cw_sb[:], cw)
         content_sb = []
         for g in range(N_GROUPS):
+            if g == HALF // GROUP:
+                nc.sync.dma_start(cw_sb[:], cw)
             group_sb = held.tile([C, GROUP, D], BF16, name=f"content_sb{g}")
             nc.sync.dma_start(group_sb[:], content[:, g * GROUP : (g + 1) * GROUP, :])
             content_sb.append(group_sb)
@@ -85,7 +89,7 @@ def tile_weightedbackpacklmheadmodel_kernel(tc, content, ctx, wg, cw, offs, out)
                         proj_ps[:, k, :], lhsT=content_t[:, b * BANK_J + k, :], rhs=wg_sb[:], start=True, stop=True
                     )
                 for k in range(BANK_J):
-                    if bank % 3 == 2:
+                    if (3 * bank) % 8 < 3:
                         relu_v = scratch.tile([C, N], BF16, name="relu_v")
                         nc.vector.tensor_scalar(
                             relu_v[:], proj_ps[:, k, :], 0.0, None, ALU.max, ALU.add, accum_out=sims[h][:, bank_h, k : k + 1]
@@ -111,21 +115,30 @@ def tile_weightedbackpacklmheadmodel_kernel(tc, content, ctx, wg, cw, offs, out)
             nc.vector.tensor_tensor(picked[:], cw_sb[:].indirect(half_of_list), scores[:], ALU.mult)
             nc.vector.scalar_tensor_tensor(weights[h][:], picked[:], 1.0, scores[:], ALU.add, ALU.subtract)
 
+        acc_ps = psum_acc.tile([N, D], F32, name="acc_ps")
+
+        def mix(g):
+            for k in range(GROUP):
+                j = g * GROUP + k
+                h, j_h = divmod(j, HALF)
+                weighted = scaled.tile([C, D], BF16, name="weighted")
+                nc.vector.tensor_scalar_mul(weighted[:], content_sb[g][:, k, :], weights[h][:, j_h : j_h + 1])
+                nc.tensor.matmul(acc_ps[:], lhsT=ctx_sb[:, :, j], rhs=weighted[:], start=(j == 0), stop=(j == N - 1))
+
         content_t = [flip(g) for g in range(AHEAD)]
         for g in range(N_GROUPS):
             if g + AHEAD < N_GROUPS:
                 content_t.append(flip(g + AHEAD))
             project(g, content_t[g])
-            if (g + 1) * GROUP % HALF == 0:
-                weigh((g + 1) * GROUP // HALF - 1)
-
-        acc_ps = psum_proj.tile([N, D], F32, name="acc_ps", tag="proj_ps")
-        for j in range(N):
-            g, k = divmod(j, GROUP)
-            h, j_h = divmod(j, HALF)
-            weighted = scaled.tile([C, D], BF16, name="weighted")
-            nc.vector.tensor_scalar_mul(weighted[:], content_sb[g][:, k, :], weights[h][:, j_h : j_h + 1])
-            nc.tensor.matmul(acc_ps[:], lhsT=ctx_sb[:, :, j], rhs=weighted[:], start=(j == 0), stop=(j == N - 1))
+            if g == HALF // GROUP - 1:
+                weigh(0)
+            if g >= MIX_FROM:
+                for m in range((g - MIX_FROM) * MIX_RATE, (g - MIX_FROM + 1) * MIX_RATE):
+                    mix(m)
+        for m in range((N_GROUPS - MIX_FROM) * MIX_RATE, N_GROUPS):
+            if m == HALF // GROUP:
+                weigh(1)
+            mix(m)
 
         acc_sb = held.tile([N, D], F32, name="acc_sb")
         nc.vector.tensor_copy(acc_sb[:], acc_ps[:])

@@ -16,8 +16,6 @@ BANK_J = 4
 BLOCK = 8
 HALF = N // 2
 AHEAD = 2
-MIX_FROM = 14
-MIX_RATE = 1
 WARM_UP = 16
 CTX_PARTS = 4
 
@@ -132,10 +130,7 @@ def tile_weightedbackpacklmheadmodel_kernel(tc, content, ctx, wg, cw, offs, out)
             project(g, content_t[g])
             if g == HALF // GROUP - 1:
                 weigh(0)
-            if g >= MIX_FROM:
-                for m in range((g - MIX_FROM) * MIX_RATE, (g - MIX_FROM + 1) * MIX_RATE):
-                    mix(m)
-        for m in range((N_GROUPS - MIX_FROM) * MIX_RATE, N_GROUPS):
+        for m in range(N_GROUPS):
             if m == HALF // GROUP:
                 weigh(1)
             mix(m)

@@ -87,7 +87,7 @@ def tile_weightedbackpacklmheadmodel_kernel(tc, content, ctx, wg, cw, offs, out)
                         proj_ps[:, k, :], lhsT=content_t[:, b * BANK_J + k, :], rhs=wg_sb[:], start=True, stop=True
                     )
                 for k in range(BANK_J):
-                    if (3 * bank) % 8 < 3:
+                    if bank % 3 == 2:
                         relu_v = scratch.tile([C, N], BF16, name="relu_v")
                         nc.vector.tensor_scalar(
                             relu_v[:], proj_ps[:, k, :], 0.0, None, ALU.max, ALU.add, accum_out=sims[h][:, bank_h, k : k + 1]

@@ -17,7 +17,7 @@ BLOCK = 8
 HALF = N // 2
 AHEAD = 2
 WARM_UP = 16
-CTX_PARTS = 4
+LOADS = (8, 8, 8, 8, 8, 8, 8, 8, 16, 16, 32)
 
 
 def tile_weightedbackpacklmheadmodel_kernel(tc, content, ctx, wg, cw, offs, out):
@@ -36,17 +36,15 @@ def tile_weightedbackpacklmheadmodel_kernel(tc, content, ctx, wg, cw, offs, out)
         wg_sb = held.tile([D, N], BF16, name="wg_sb")
         nc.scalar.dma_start(wg_sb[:], wg)
         cw_sb = held.tile([C, S], F32, name="cw_sb")
-        content_sb = []
-        for g in range(N_GROUPS):
-            if g == HALF // GROUP:
+        block = []
+        for p, positions in enumerate(LOADS):
+            if len(block) == HALF:
                 nc.sync.dma_start(cw_sb[:], cw)
-            group_sb = held.tile([C, GROUP, D], BF16, name=f"content_sb{g}")
-            nc.sync.dma_start(group_sb[:], content[:, g * GROUP : (g + 1) * GROUP, :])
-            content_sb.append(group_sb)
+            piece_sb = held.tile([C, positions, D], BF16, name=f"content_sb{p}")
+            nc.sync.dma_start(piece_sb[:], content[:, len(block) : len(block) + positions, :])
+            block.extend([piece_sb[:, k, :] for k in range(positions)])
         ctx_sb = held.tile([C, N, N], BF16, name="ctx_sb")
-        rows = N // CTX_PARTS
-        for q in range(CTX_PARTS):
-            nc.sync.dma_start(ctx_sb[:, q * rows : (q + 1) * rows, :], ctx[:, q * rows : (q + 1) * rows, :])
+        nc.sync.dma_start(ctx_sb[:], ctx)
 
         ident_bf = held.tile([C, C], BF16, name="ident_bf")
         make_identity(nc, ident_bf[:])
@@ -72,7 +70,7 @@ def tile_weightedbackpacklmheadmodel_kernel(tc, content, ctx, wg, cw, offs, out)
         def flip(g):
             flip_ps = psum_flip.tile([D, GROUP, C], BF16, name="flip_ps")
             for k in range(GROUP):
-                nc.tensor.transpose(flip_ps[:, k, :], content_sb[g][:, k, :], ident_bf[:])
+                nc.tensor.transpose(flip_ps[:, k, :], block[g * GROUP + k], ident_bf[:])
             content_t = flipped.tile([D, GROUP, C], BF16, name="content_t")
             nc.vector.tensor_copy(content_t[:], flip_ps[:])
             return content_t
@@ -120,7 +118,7 @@ def tile_weightedbackpacklmheadmodel_kernel(tc, content, ctx, wg, cw, offs, out)
                 j = g * GROUP + k
                 h, j_h = divmod(j, HALF)
                 weighted = scaled.tile([C, D], BF16, name="weighted")
-                nc.vector.tensor_scalar_mul(weighted[:], content_sb[g][:, k, :], weights[h][:, j_h : j_h + 1])
+                nc.vector.tensor_scalar_mul(weighted[:], block[j], weights[h][:, j_h : j_h + 1])
                 nc.tensor.matmul(acc_ps[:], lhsT=ctx_sb[:, :, j], rhs=weighted[:], start=(j == 0), stop=(j == N - 1))
 
         content_t = [flip(g) for g in range(AHEAD)]

@@ -16,6 +16,7 @@ BANK_J = 4
 BLOCK = 8
 HALF = N // 2
 AHEAD = 2
+SQUARE = 32
 WARM_UP = 16
 LOADS = (8, 8, 8, 8, 8, 8, 8, 8, 16, 16, 32)
 
@@ -48,8 +49,6 @@ def tile_weightedbackpacklmheadmodel_kernel(tc, content, ctx, wg, cw, offs, out)
 
         ident_bf = held.tile([C, C], BF16, name="ident_bf")
         make_identity(nc, ident_bf[:])
-        ident_f32 = held.tile([N, N], F32, name="ident_f32")
-        make_identity(nc, ident_f32[:])
         position = held.tile([C, N], I32, name="position")
         nc.gpsimd.iota(position[:], pattern=[[1, N]], base=0, channel_multiplier=0)
         ramp = held.tile([C, N], F32, name="ramp")
@@ -133,10 +132,12 @@ def tile_weightedbackpacklmheadmodel_kernel(tc, content, ctx, wg, cw, offs, out)
                 weigh(1)
             mix(m)
 
-        acc_sb = held.tile([N, D], F32, name="acc_sb")
-        nc.vector.tensor_copy(acc_sb[:], acc_ps[:])
-        out_ps = psum_flip.tile([D, N], F32, name="out_ps", tag="flip_ps")
-        nc.tensor.transpose(out_ps[:], acc_sb[:], ident_f32[:])
-        out_sb = held.tile([D, N], F32, name="out_sb")
-        nc.vector.tensor_copy(out_sb[:], out_ps[:])
-        nc.sync.dma_start(out, out_sb[:])
+        turned = held.tile([N, D], F32, name="turned", align_bytes=64)
+        nc.vector.transpose(turned[:], acc_ps[:])
+        out_blocks = out.rearrange("(b s) i -> s b i", s=SQUARE)
+        for a in range(N // SQUARE):
+            queue = nc.sync if a % 2 == 0 else nc.scalar
+            queue.dma_start(
+                out_blocks[:, :, a * SQUARE : (a + 1) * SQUARE],
+                turned[a * SQUARE : (a + 1) * SQUARE, :].rearrange("s (b r) -> s b r", r=SQUARE),
+            )

@@ -121,7 +121,9 @@ def tile_weightedbackpacklmheadmodel_kernel(tc, content, ctx, wg, cw, offs, out)
                 nc.tensor.matmul(acc_ps[:], lhsT=ctx_sb[:, :, j], rhs=weighted[:], start=(j == 0), stop=(j == N - 1))
 
         content_t = [flip(g) for g in range(AHEAD)]
-        for g in range(N_GROUPS):
+        project(0, content_t[0])
+        content_t.append(flip(AHEAD))
+        for g in range(1, N_GROUPS):
             if g + AHEAD < N_GROUPS:
                 content_t.append(flip(g + AHEAD))
             project(g, content_t[g])

@@ -117,7 +117,11 @@ def tile_weightedbackpacklmheadmodel_kernel(tc, content, ctx, wg, cw, offs, out)
                 j = g * GROUP + k
                 h, j_h = divmod(j, HALF)
                 weighted = scaled.tile([C, D], BF16, name="weighted")
-                nc.vector.tensor_scalar_mul(weighted[:], block[j], weights[h][:, j_h : j_h + 1])
+                weight = weights[h][:, j_h : j_h + 1]
+                if g == 0:
+                    nc.gpsimd.tensor_scalar(weighted[:], block[j], weight, 1.0, ALU.mult, ALU.mult)
+                else:
+                    nc.vector.tensor_scalar_mul(weighted[:], block[j], weight)
                 nc.tensor.matmul(acc_ps[:], lhsT=ctx_sb[:, :, j], rhs=weighted[:], start=(j == 0), stop=(j == N - 1))
 
         content_t = [flip(g) for g in range(AHEAD)]

@@ -32,13 +32,14 @@ def tile_weightedbackpacklmheadmodel_kernel(tc, content, ctx, wg, cw, offs, out)
         tc.psum_pool(name="psum_proj", bufs=5) as psum_proj,
         tc.psum_pool(name="psum_acc", bufs=1) as psum_acc,
     ):
-        offsets = held.tile([C, N // 16], U16, name="offsets")
-        nc.sync.dma_start(offsets[:], offs)
         wg_sb = held.tile([D, N], BF16, name="wg_sb")
         nc.scalar.dma_start(wg_sb[:], wg)
+        offsets = held.tile([C, N // 16], U16, name="offsets")
         cw_sb = held.tile([C, S], F32, name="cw_sb")
         block = []
         for p, positions in enumerate(LOADS):
+            if len(block) == AHEAD * GROUP:
+                nc.sync.dma_start(offsets[:], offs)
             if len(block) == HALF:
                 nc.sync.dma_start(cw_sb[:], cw)
             piece_sb = held.tile([C, positions, D], BF16, name=f"content_sb{p}")
@@ -71,7 +72,10 @@ def tile_weightedbackpacklmheadmodel_kernel(tc, content, ctx, wg, cw, offs, out)
             for k in range(GROUP):
                 nc.tensor.transpose(flip_ps[:, k, :], block[g * GROUP + k], ident_bf[:])
             content_t = flipped.tile([D, GROUP, C], BF16, name="content_t")
-            nc.vector.tensor_copy(content_t[:], flip_ps[:])
+            copies = GROUP // BANK_J if g == 0 else 1
+            size = GROUP // copies
+            for k in range(copies):
+                nc.vector.tensor_copy(content_t[:, k * size : (k + 1) * size, :], flip_ps[:, k * size : (k + 1) * size, :])
             return content_t
 
         def project(g, content_t):

@@ -60,9 +60,11 @@ def tile_weightedbackpacklmheadmodel_kernel(tc, content, ctx, wg, cw, offs, out)
         table_out = held.tile([C, 1], F32, name="table_out")
         nc.scalar.activation(table_out[:], table_in[:], ACT.Sigmoid)
 
+        zeros = held.tile([C, N], BF16, name="zeros")
+        nc.vector.memset(zeros[:], 0.0)
         warm_ps = psum_proj.tile([C, BANK_J, N], F32, name="warm_ps", tag="proj_ps")
         for w in range(WARM_UP):
-            nc.tensor.matmul(warm_ps[:, w % BANK_J, :], lhsT=ident_bf[:], rhs=ident_bf[:], start=True, stop=True)
+            nc.tensor.matmul(warm_ps[:, w % BANK_J, :], lhsT=zeros[:], rhs=zeros[:], start=True, stop=True)
 
         sims = [held.tile([C, HALF // BANK_J, BLOCK], F32, name=f"sims{h}") for h in range(2)]
         weights = [held.tile([C, HALF], F32, name=f"weights{h}") for h in range(2)]

import concourse.mybir as mybir
from concourse.masks import make_identity

C, S, N, D = 128, 1024, 128, 128
ANNEAL, SHIFT, NEAR = 0.1, 6.0, 100.0
FLOPS = 2 * (2 * C * N * D * N)

BF16, F32 = mybir.dt.bfloat16, mybir.dt.float32
I32, U16 = mybir.dt.int32, mybir.dt.uint16
ALU = mybir.AluOpType
ACT = mybir.ActivationFunctionType

GROUP = 8
N_GROUPS = N // GROUP
BANK_J = 4
BLOCK = 8
HALF = N // 2
AHEAD = 2
SQUARE = 32
WARM_UP = 16
LOADS = (8, 8, 8, 8, 8, 8, 8, 8, 16, 16, 32)


def tile_weightedbackpacklmheadmodel_kernel(tc, content, ctx, wg, cw, offs, out):
    nc = tc.nc
    with (
        tc.tile_pool(name="held", bufs=1) as held,
        tc.tile_pool(name="flipped", bufs=AHEAD + 2) as flipped,
        tc.tile_pool(name="scratch", bufs=2) as scratch,
        tc.tile_pool(name="scaled", bufs=2 * GROUP) as scaled,
        tc.psum_pool(name="psum_flip", bufs=2) as psum_flip,
        tc.psum_pool(name="psum_proj", bufs=5) as psum_proj,
        tc.psum_pool(name="psum_acc", bufs=1) as psum_acc,
    ):
        wg_sb = held.tile([D, N], BF16, name="wg_sb")
        nc.scalar.dma_start(wg_sb[:], wg)
        offsets = held.tile([C, N // 16], U16, name="offsets")
        cw_sb = held.tile([C, S], F32, name="cw_sb")
        block = []
        for p, positions in enumerate(LOADS):
            if len(block) == AHEAD * GROUP:
                nc.sync.dma_start(offsets[:], offs)
            if len(block) == HALF:
                nc.sync.dma_start(cw_sb[:], cw)
            piece_sb = held.tile([C, positions, D], BF16, name=f"content_sb{p}")
            nc.sync.dma_start(piece_sb[:], content[:, len(block) : len(block) + positions, :])
            block.extend([piece_sb[:, k, :] for k in range(positions)])
        ctx_sb = held.tile([C, N, N], BF16, name="ctx_sb")
        nc.sync.dma_start(ctx_sb[:], ctx)

        ident_bf = held.tile([C, C], BF16, name="ident_bf")
        make_identity(nc, ident_bf[:])
        position = held.tile([C, N], I32, name="position")
        nc.gpsimd.iota(position[:], pattern=[[1, N]], base=0, channel_multiplier=0)
        ramp = held.tile([C, N], F32, name="ramp")
        nc.vector.tensor_scalar(ramp[:], position[:], 1.0 / NEAR, 1.0, ALU.mult, ALU.add)

        table_in = held.tile([C, 1], F32, name="table_in")
        nc.vector.memset(table_in[:], 0.0)
        table_out = held.tile([C, 1], F32, name="table_out")
        nc.scalar.activation(table_out[:], table_in[:], ACT.Sigmoid)

        zeros = held.tile([C, N], BF16, name="zeros")
        nc.vector.memset(zeros[:], 0.0)
        warm_ps = psum_proj.tile([C, BANK_J, N], F32, name="warm_ps", tag="proj_ps")
        for w in range(WARM_UP):
            nc.tensor.matmul(warm_ps[:, w % BANK_J, :], lhsT=zeros[:], rhs=zeros[:], start=True, stop=True)

        sims = [held.tile([C, HALF // BANK_J, BLOCK], F32, name=f"sims{h}") for h in range(2)]
        weights = [held.tile([C, HALF], F32, name=f"weights{h}") for h in range(2)]

        def flip(g):
            flip_ps = psum_flip.tile([D, GROUP, C], BF16, name="flip_ps")
            for k in range(GROUP):
                nc.tensor.transpose(flip_ps[:, k, :], block[g * GROUP + k], ident_bf[:])
            content_t = flipped.tile([D, GROUP, C], BF16, name="content_t")
            copies = GROUP // BANK_J if g == 0 else 1
            size = GROUP // copies
            for k in range(copies):
                nc.vector.tensor_copy(content_t[:, k * size : (k + 1) * size, :], flip_ps[:, k * size : (k + 1) * size, :])
            return content_t

        def project(g, content_t):
            for b in range(GROUP // BANK_J):
                bank = g * (GROUP // BANK_J) + b
                h, bank_h = divmod(bank, HALF // BANK_J)
                proj_ps = psum_proj.tile([C, BANK_J, N], F32, name="proj_ps")
                for k in range(BANK_J):
                    nc.tensor.matmul(
                        proj_ps[:, k, :], lhsT=content_t[:, b * BANK_J + k, :], rhs=wg_sb[:], start=True, stop=True
                    )
                for k in range(BANK_J):
                    if bank % 3 == 2:
                        relu_v = scratch.tile([C, N], BF16, name="relu_v")
                        nc.vector.tensor_scalar(
                            relu_v[:], proj_ps[:, k, :], 0.0, None, ALU.max, ALU.add, accum_out=sims[h][:, bank_h, k : k + 1]
                        )
                    else:
                        relu_s = scratch.tile([C, N], BF16, name="relu_s")
                        nc.scalar.activation(
                            relu_s[:], proj_ps[:, k, :], ACT.Relu, accum_out=sims[h][:, bank_h, k : k + 1]
                        )

        def weigh(h):
            scores = held.tile([C, HALF], F32, name=f"scores{h}")
            nc.scalar.activation(
                scores[:].rearrange("c (b k) -> c b k", k=BANK_J),
                sims[h][:, :, 0:BANK_J],
                ACT.Sigmoid,
                bias=SHIFT,
                scale=-ANNEAL,
            )
            nc.vector.tensor_tensor(scores[:], scores[:], ramp[:, h * HALF : (h + 1) * HALF], ALU.mult)
            picked = held.tile([C, HALF], F32, name=f"picked{h}")
            half_of_list = offsets[:, h * (HALF // 16) : (h + 1) * (HALF // 16)]
            nc.vector.tensor_tensor(picked[:], cw_sb[:].indirect(half_of_list), scores[:], ALU.mult)
            nc.vector.scalar_tensor_tensor(weights[h][:], picked[:], 1.0, scores[:], ALU.add, ALU.subtract)

        acc_ps = psum_acc.tile([N, D], F32, name="acc_ps")

        def mix(g):
            for k in range(GROUP):
                j = g * GROUP + k
                h, j_h = divmod(j, HALF)
                weighted = scaled.tile([C, D], BF16, name="weighted")
                weight = weights[h][:, j_h : j_h + 1]
                if g == 0:
                    nc.gpsimd.tensor_scalar(weighted[:], block[j], weight, 1.0, ALU.mult, ALU.mult)
                else:
                    nc.vector.tensor_scalar_mul(weighted[:], block[j], weight)
                nc.tensor.matmul(acc_ps[:], lhsT=ctx_sb[:, :, j], rhs=weighted[:], start=(j == 0), stop=(j == N - 1))

        content_t = [flip(g) for g in range(AHEAD)]
        project(0, content_t[0])
        content_t.append(flip(AHEAD))
        for g in range(1, N_GROUPS):
            if g + AHEAD < N_GROUPS:
                content_t.append(flip(g + AHEAD))
            project(g, content_t[g])
            if g == HALF // GROUP - 1:
                weigh(0)
        for m in range(N_GROUPS):
            if m == HALF // GROUP:
                weigh(1)
            mix(m)

        turned = held.tile([N, D], F32, name="turned", align_bytes=64)
        nc.vector.transpose(turned[:], acc_ps[:])
        out_blocks = out.rearrange("(b s) i -> s b i", s=SQUARE)
        for a in range(N // SQUARE):
            queue = nc.sync if a % 2 == 0 else nc.scalar
            queue.dma_start(
                out_blocks[:, :, a * SQUARE : (a + 1) * SQUARE],
                turned[a * SQUARE : (a + 1) * SQUARE, :].rearrange("s (b r) -> s b r", r=SQUARE),
            )
